import numpy as np
import ml_dtypes


def mxq(x, axis, fmt="e4m3"):
    dtype, down = {"e4m3": (ml_dtypes.float8_e4m3fn, 7), "e5m2": (ml_dtypes.float8_e5m2, 14)}[fmt]
    v = np.moveaxis(np.asarray(x, np.float32).astype(ml_dtypes.bfloat16).astype(np.float64), axis, -1)
    blocks = v.reshape(v.shape[:-1] + (-1, 32))
    amax = np.abs(blocks).max(-1, keepdims=True)
    byte = np.maximum(np.where(amax > 0, np.frexp(amax)[1] - 1 + 127, 0) - down, 1)
    scale = np.exp2(byte - 127.0)
    codes = (blocks / scale).astype(np.float32).astype(dtype).astype(np.float64)
    return np.moveaxis((codes * scale).reshape(v.shape), -1, axis)


WIDE = False


def mx_kscale(k):
    if not WIDE:
        return np.ones(k)
    levels = np.array([18, -18])
    if k % 512:
        return np.exp2(np.random.permutation(np.resize(levels, k // 32))).repeat(32)
    a = np.empty((k // 512, 16))
    for p in range(k // 512):
        a[p, :8] = np.random.permutation(np.resize(levels, 8))
        for g in range(8):
            far = levels[np.abs(levels - a[p, g]) >= 10]
            a[p, g + 8] = far[np.random.randint(len(far))]
    return np.exp2(a.ravel()).repeat(32)


BF16 = ml_dtypes.bfloat16


def bf(x):
    return np.asarray(x, np.float32).astype(BF16)


def f64(x):
    return np.asarray(x).astype(np.float64)


B, S, D, H, KVH, HD = 1, 1024, 768, 16, 4, 128
E = H * HD
KV = KVH * HD
T = B * S
EPS = 1e-6


def norm_rope_backward(g, z, cos, sin, gamma, n):
    half = HD // 2
    w = g * sin[None, None]
    du = g * cos[None, None] + np.concatenate([w[..., half:], -w[..., :half]], axis=-1)
    dn = (du * gamma).transpose(0, 2, 1, 3)
    zh = z.reshape(B, S, n, HD)
    c = zh - zh.mean(-1, keepdims=True)
    r = 1.0 / np.sqrt(np.square(c).mean(-1, keepdims=True) + EPS)
    zn = c * r
    dz = r * (dn - dn.mean(-1, keepdims=True) - zn * (dn * zn).mean(-1, keepdims=True))
    return dz.reshape(T, n * HD)


def setup_inputs():
    s = mx_kscale(S)
    uh = mx_kscale(E + KV)[::96][:H + KVH]
    uq = np.repeat(uh[:H], HD)
    uk = np.repeat(uh[H:], HD)
    uv = mx_kscale(KV)
    x0 = bf(np.random.standard_normal((B, S, D)))
    cos = bf(np.random.uniform(size=(S, HD)))
    sin = bf(np.random.uniform(size=(S, HD)))
    wq0 = bf(np.random.standard_normal((D, E)) / np.sqrt(D))
    wk0 = bf(np.random.standard_normal((D, KV)) / np.sqrt(D))
    wv0 = bf(np.random.standard_normal((D, KV)) * 2.0 / np.sqrt(D))
    q_gamma = bf(1.0 + 0.1 * np.random.standard_normal(HD))
    q_beta = bf(0.1 * np.random.standard_normal(HD))
    k_gamma = bf(1.0 + 0.1 * np.random.standard_normal(HD))
    k_beta = bf(0.1 * np.random.standard_normal(HD))
    zq = f64(x0) @ f64(wq0)
    zk = f64(x0) @ f64(wk0)
    st = s[None, None, :, None]
    g0 = np.random.standard_normal((B, H, S, HD)) * np.exp2(np.random.randint(-6, 1, (B, 1, S, 1)))
    g1 = np.random.standard_normal((B, KVH, S, HD)) * np.exp2(np.random.randint(-6, 1, (B, 1, S, 1)))
    g2 = np.random.standard_normal((B, KVH, S, HD)) * np.exp2(np.random.randint(-6, 1, (B, 1, S, 1)))
    return {
        "x": bf(f64(x0) * s[None, :, None]),
        "cos": cos,
        "sin": sin,
        "Wq": bf(f64(wq0) / uq),
        "Wk": bf(f64(wk0) / uk),
        "Wv": bf(f64(wv0) / uv),
        "q_gamma": q_gamma,
        "q_beta": q_beta,
        "k_gamma": k_gamma,
        "k_beta": k_beta,
        "zq": np.asarray(zq, np.float32),
        "zk": np.asarray(zk, np.float32),
        "grad_0": bf(g0 / st * uq.reshape(1, H, 1, HD)),
        "grad_1": bf(g1 / st * uk.reshape(1, KVH, 1, HD)),
        "grad_2": bf(g2 / st * uv.reshape(1, KVH, 1, HD)),
    }


def reference(x, cos, sin, Wq, Wk, Wv, q_gamma, q_beta, k_gamma, k_beta, zq, zk, grad_0, grad_1, grad_2):
    c, sn = f64(cos), f64(sin)
    dq = norm_rope_backward(f64(grad_0), f64(zq), c, sn, f64(q_gamma), H)
    dk = norm_rope_backward(f64(grad_1), f64(zk), c, sn, f64(k_gamma), KVH)
    dv = f64(grad_2).transpose(0, 2, 1, 3).reshape(T, KV)
    dz = np.concatenate([dq, dk, dv], axis=1)
    w = np.concatenate([f64(Wq), f64(Wk), f64(Wv)], axis=1)
    dx = (mxq(dz, 1, "e5m2") @ mxq(w, 1, "e4m3").T).reshape(B, S, D)
    dw = mxq(f64(x).reshape(T, D), 0, "e4m3").T @ mxq(dz, 0, "e5m2")
    return dx, dw[:, :E], dw[:, E:E + KV], dw[:, E + KV:]

@@ -1,0 +1,629 @@
+from contextlib import ExitStack
+
+import concourse.mybir as mybir
+from concourse.masks import make_identity
+
+F32 = mybir.dt.float32
+BF16 = mybir.dt.bfloat16
+U32 = mybir.dt.uint32
+U8 = mybir.dt.uint8
+E4M3 = mybir.dt.float8_e4m3fn_x4
+E5M2 = mybir.dt.float8_e5m2_x4
+ALU = mybir.AluOpType
+ACT = mybir.ActivationFunctionType
+AX = mybir.AxisListType
+
+P = 128
+T = 1024
+D = 768
+HD = 128
+EPS = 1e-6
+NG = 2
+NH = 6
+FLOPS = 2 * 2 * T * D * 3072
+
+
+def tile_gqa_flashattn_pa_v_kernel(
+    tc, x, cos, sin, wq, wk, wv, q_gamma, q_beta, k_gamma, k_beta, zq, zk, grad_0, grad_1, grad_2,
+    out_0, out_1, out_2, out_3,
+):
+    nc = tc.nc
+    x_v = x[0].rearrange("(g p j) d -> g p j d", p=P, j=4)
+    cos_v = cos.rearrange("(g p j) f -> g p j f", p=P, j=4)
+    sin_v = sin.rearrange("(g p j) f -> g p j f", p=P, j=4)
+    zq_v = zq[0].rearrange("(g p j) c -> g p j c", p=P, j=4)
+    zk_v = zk[0].rearrange("(g p j) c -> g p j c", p=P, j=4)
+    g0_v = grad_0[0].rearrange("h (g p j) f -> g p h (j f)", p=P, j=4)
+    g1_v = grad_1[0].rearrange("h (g p j) f -> g p h (j f)", p=P, j=4)
+    g2_v = grad_2[0].rearrange("h (g p j) f -> g h p j f", p=P, j=4)
+    dx_v = out_0[0].rearrange("(g p j) d -> g p j d", p=P, j=4)
+
+    def z_src(g, hg):
+        return zq_v[g][:, :, hg * 512 : (hg + 1) * 512] if hg < 4 else zk_v[g]
+
+    def g_src(g, hg):
+        return g0_v[g][:, hg * 4 : hg * 4 + 4, :] if hg < 4 else g1_v[g]
+
+    def dw_dst(hg, d):
+        rows = slice(d * P, (d + 1) * P)
+        if hg < 4:
+            return out_1[rows, hg * 512 : (hg + 1) * 512]
+        return out_2[rows, :] if hg == 4 else out_3[rows, :]
+
+    with ExitStack() as ctx:
+        const = ctx.enter_context(tc.tile_pool(name="const", bufs=1))
+        work = ctx.enter_context(tc.tile_pool(name="work", bufs=3))
+        codes = ctx.enter_context(tc.tile_pool(name="codes", bufs=1))
+        ps = ctx.enter_context(tc.psum_pool(name="ps", bufs=1))
+
+        ident = const.tile([P, P], F32, name="ident")
+        make_identity(nc, ident[:])
+        sel = const.tile([P, 16], F32, name="sel")
+        sel1 = const.tile([P, 16], F32, name="sel1")
+        nc.vector.tensor_reduce(out=sel1[:], in_=ident[:].rearrange("p (n e) -> p n e", e=8), axis=AX.X, op=ALU.add)
+        nc.vector.tensor_scalar(out=sel[:], in0=sel1[:], scalar1=1.0 / HD, scalar2=None, op0=ALU.mult)
+        zero = const.tile([P, 1], F32, name="zero")
+        nc.vector.memset(zero[:], 0.0)
+        eps = const.tile([P, 1], F32, name="eps")
+        nc.vector.tensor_scalar(out=eps[:], in0=zero[:], scalar1=EPS, scalar2=None, op0=ALU.add)
+
+        units = [(0, 0), (1, 0), (0, 1), (0, 2), (0, 3), (0, 4), (1, 1), (1, 2), (1, 3), (1, 4)]
+        cosr = [None, None]
+        sinr = [None, None]
+        gam = {}
+        gsw = {}
+        tab = {}
+        zt = {}
+        gt = {}
+
+        def load_cs(g):
+            a = const.tile([P, 4, HD], BF16, name="cosr%d" % g)
+            nc.sync.dma_start(out=a[:], in_=cos_v[g])
+            b = const.tile([P, 4, HD], BF16, name="sinr%d" % g)
+            nc.sync.dma_start(out=b[:], in_=sin_v[g])
+            cosr[g] = a
+            sinr[g] = b
+
+        def load_gamma(kind, src):
+            a = const.tile([P, HD], BF16, name="gam_" + kind, tag="gam_" + kind)
+            nc.sync.dma_start(out=a[:], in_=src.partition_broadcast(P))
+            gam[kind] = a
+
+        def swap_gamma(kind):
+            a = gam[kind]
+            b = const.tile([P, HD], BF16, name="gsw_" + kind, tag="gsw_" + kind)
+            nc.vector.tensor_scalar(out=b[:, 0:64], in0=a[:, 64:128], scalar1=-1.0, scalar2=None, op0=ALU.mult)
+            nc.vector.tensor_copy(out=b[:, 64:128], in_=a[:, 0:64])
+            gsw[kind] = b
+
+        def make_tables(g, kind):
+            a, b = gam[kind], gsw[kind]
+            c = const.tile([P, 4, HD], F32, name="tab_c%d" % g)
+            s = const.tile([P, 4, HD], F32, name="tab_s%d" % g)
+            nc.vector.tensor_tensor(out=c[:], in0=cosr[g][:], in1=a[:].unsqueeze(1).to_broadcast([P, 4, HD]), op=ALU.mult)
+            nc.vector.tensor_tensor(out=s[:], in0=sinr[g][:], in1=b[:].unsqueeze(1).to_broadcast([P, 4, HD]), op=ALU.mult)
+            tab[(g, kind)] = (c, s)
+
+        def load_unit(n):
+            g, hg = units[n]
+            b = work.tile([P, 4, 512], BF16, name="gt", tag="gt", bufs=2)
+            nc.sync.dma_start(out=b[:], in_=g_src(g, hg))
+            a = work.tile([P, 4, 512], F32, name="zt", tag="zt", bufs=4)
+            nc.sync.dma_start(out=a[:], in_=z_src(g, hg))
+            gt[n] = b
+            zt[n] = a
+
+        xc = codes.tile([P, NG, D], U32, name="xc", align_bytes=64)
+        xs = codes.tile([P, NG, D], U8, name="xs", align_bytes=64)
+        wc = codes.tile([P, NH, D], U32, name="wc", align_bytes=64)
+        ws = codes.tile([P, NH, D], U8, name="ws", align_bytes=64)
+        fc = {}
+        fs = {}
+        tcd = {}
+        tsc = {}
+        for hg in range(NH):
+            for g in range(NG):
+                fc[(g, hg)] = codes.tile([P, 512], U32, name="fc%d_%d" % (g, hg), align_bytes=64)
+                fs[(g, hg)] = codes.tile([P, 512], U8, name="fs%d_%d" % (g, hg), align_bytes=64)
+
+        def token_codes(g, hg):
+            tcd[(g, hg)] = work.tile([P, 512], U32, name="tcod", tag="tcod", bufs=6, align_bytes=64)
+            tsc[(g, hg)] = work.tile([P, 512], U8, name="tsca", tag="tsca", bufs=6, align_bytes=64)
+            return tcd[(g, hg)], tsc[(g, hg)]
+
+        def interleave(engine_copy, dst, src):
+            engine_copy(
+                out=dst.rearrange("p (c i) t -> p c t i", i=4),
+                in_=src.rearrange("p t (c i) -> p c t i", i=4),
+            )
+
+        xraw = {}
+
+        def load_x(g):
+            for lo, w in ((0, 512), (512, 256)):
+                raw = work.tile([P, 4, w], BF16, name="raw", tag="raw", bufs=4)
+                nc.sync.dma_start(out=raw[:], in_=x_v[g][:, :, lo : lo + w])
+                xraw[(g, lo)] = raw
+
+        def prep_x(g):
+            for lo, w, tag, bufs in ((0, 512, "q", 3), (512, 256, "wil", 4)):
+                il = work.tile([P, w, 4], BF16, name="xil", tag=tag, bufs=bufs, align_bytes=64)
+                interleave(nc.scalar.copy, il[:], xraw[(g, lo)][:])
+                yield_q(g, lo, w, il)
+
+        xq = []
+
+        def yield_q(g, lo, w, il):
+            def f():
+                nc.vector.quantize_mx(
+                    out=xc[:, g, lo : lo + w].bitcast(E4M3),
+                    scales=xs[:, g, lo : lo + w],
+                    in_=il[:].rearrange("p c j -> p (c j)"),
+                )
+
+            xq.append(f)
+
+        wraw = {}
+
+        def load_w(dp, c):
+            raw = work.tile([P, 2, 1024], BF16, name="raw", tag="raw", bufs=4)
+            rows = slice(dp * 256, dp * 256 + 256)
+            if c < 2:
+                nc.sync.dma_start(
+                    out=raw[:], in_=wq[rows, c * 1024 : (c + 1) * 1024].rearrange("(k p) e -> p k e", p=P)
+                )
+            else:
+                nc.sync.dma_start(out=raw[:, :, 0:512], in_=wk[rows, :].rearrange("(k p) e -> p k e", p=P))
+                nc.sync.dma_start(out=raw[:, :, 512:1024], in_=wv[rows, :].rearrange("(k p) e -> p k e", p=P))
+            wraw[(dp, c)] = raw
+
+        def w_job(dp, hg):
+            bank = ps.tile([P, 2, 2, P], F32, name="tr", tag="tr", bufs=2)
+            for k in range(2):
+                words = wraw[(dp, hg // 2)][:, k, :].bitcast(F32)
+                lo = (hg % 2) * 256
+                for u in range(2):
+                    nc.tensor.transpose(bank[:, k, u, :], words[:, lo + u : lo + 256 : 2], ident[:])
+            il = work.tile([P, 2, P, 4], BF16, name="wil", tag="wil", bufs=4, align_bytes=64)
+            nc.scalar.copy(
+                out=il[:].rearrange("p k r e -> p (k r e)").bitcast(F32).rearrange("p (k r u) -> p k r u", k=2, u=2),
+                in_=bank[:].rearrange("p k u r -> p k r u"),
+            )
+
+            def fin():
+                cols = slice(dp * 256, dp * 256 + 256)
+                nc.vector.quantize_mx(
+                    out=wc[:, hg, cols].bitcast(E4M3),
+                    scales=ws[:, hg, cols],
+                    in_=il[:].rearrange("p k r e -> p (k r e)"),
+                )
+
+            return fin
+
+        def f_transposes(dz):
+            banks = []
+            for jp in range(2):
+                bank = ps.tile([P, 2, 2, P], F32, name="tr", tag="tr", bufs=2)
+                for k in range(2):
+                    words = dz[:, jp * 2 + k, :].bitcast(F32)
+                    for u in range(2):
+                        nc.tensor.transpose(bank[:, k, u, :], words[:, u:256:2], ident[:])
+                banks.append(bank)
+            return banks
+
+        def f_copies(banks, second=nc.scalar.copy):
+            xt = work.tile([P, 4, P, 4], BF16, name="xt", tag="q", bufs=3, align_bytes=64)
+            for jp in range(2):
+                dst = xt[:, jp * 2 : jp * 2 + 2].rearrange("p k r e -> p (k r e)").bitcast(F32)
+                (second if jp else nc.scalar.copy)(
+                    out=dst.rearrange("p (k r u) -> p k r u", k=2, u=2),
+                    in_=banks[jp][:].rearrange("p k u r -> p k r u"),
+                )
+            return xt
+
+        def quant_f(g, hg, xt):
+            nc.vector.quantize_mx(
+                out=fc[(g, hg)][:].bitcast(E5M2), scales=fs[(g, hg)][:], in_=xt[:].rearrange("p k r e -> p (k r e)")
+            )
+
+        def quant_t(g, hg, il):
+            c, s = token_codes(g, hg)
+            nc.vector.quantize_mx(out=c[:].bitcast(E5M2), scales=s[:], in_=il[:].rearrange("p c j -> p (c j)"))
+
+        def load_dv(g):
+            dz = work.tile([P, 4, 512], BF16, name="dz", tag="dz", bufs=2)
+            for h in range(4):
+                nc.sync.dma_start(out=dz[:, :, h * HD : (h + 1) * HD], in_=g2_v[g][h])
+            return dz
+
+        def dv_unit(g, dz):
+            il = work.tile([P, 512, 4], BF16, name="il", tag="q", bufs=3, align_bytes=64)
+            interleave(nc.scalar.copy, il[:], dz[:])
+            xt = f_copies(f_transposes(dz))
+
+            def fin():
+                quant_t(g, 5, il)
+                quant_f(g, 5, xt)
+
+            return fin
+
+        dwn = [0]
+        dwt = {}
+
+        def dw_job(hg, d):
+            acc = ps.tile([P, 512], F32, name="mm", tag="mm", bufs=4)
+            for g in range(NG):
+                nc.tensor.matmul_mx(
+                    out=acc[:],
+                    lhsT=xc[:, g, d * P : (d + 1) * P].bitcast(E4M3),
+                    lhsT_scale=xs[:, g, d * P : (d + 1) * P],
+                    rhs=tcd[(g, hg)][:].bitcast(E5M2),
+                    rhs_scale=tsc[(g, hg)][:],
+                    start=(g == 0),
+                    stop=(g == NG - 1),
+                )
+
+            def fin(copy):
+                if hg in (5, 0):
+                    o = work.tile([P, 512], F32, name="dwo", tag="dwo", bufs=4)[:]
+                else:
+                    if dwn[0] % 2 == 0:
+                        dwt[0] = work.tile([P, 2, 512], F32, name="dwo2", tag="raw", bufs=4)
+                    o = dwt[0][:, dwn[0] % 2, :]
+                    dwn[0] += 1
+                copy(out=o, in_=acc[:])
+                nc.sync.dma_start(out=dw_dst(hg, d), in_=o)
+
+            return fin
+
+        dxo = {}
+        order = (5, 0, 1, 2, 3, 4)
+
+        def dx_open(g, j, half, tag="mm", bufs=4):
+            acc = ps.tile([P, 512], F32, name="mm", tag=tag, bufs=bufs)
+
+            def mm(k, start, stop):
+                hg = order[k]
+                nc.tensor.matmul_mx(
+                    out=acc[:],
+                    lhsT=fc[(g, hg)][:, j * P : (j + 1) * P].bitcast(E5M2),
+                    lhsT_scale=fs[(g, hg)][:, j * P : (j + 1) * P],
+                    rhs=wc[:, hg, half * 256 : half * 256 + 512].bitcast(E4M3),
+                    rhs_scale=ws[:, hg, half * 256 : half * 256 + 512],
+                    start=start,
+                    stop=stop,
+                )
+
+            for k in range(5):
+                mm(k, k == 0, False)
+
+            def close():
+                mm(5, False, True)
+
+                def fin(copy):
+                    if half == 0:
+                        dxo[(g, j)] = work.tile([P, D], F32, name="dxo", tag="dxo", bufs=3)
+                        copy(out=dxo[(g, j)][:, 0:512], in_=acc[:])
+                    else:
+                        copy(out=dxo[(g, j)][:, 512:768], in_=acc[:, 256:512])
+                        nc.sync.dma_start(out=dx_v[g][:, j, :], in_=dxo[(g, j)][:])
+
+                return fin
+
+            return close
+
+        def dx_job(g, j, half):
+            return dx_open(g, j, half)()
+
+        def dx_part(g, j, half, ks):
+            acc = ps.tile([P, 512], F32, name="mm", tag="mm", bufs=4)
+            for k in ks:
+                hg = order[k]
+                nc.tensor.matmul_mx(
+                    out=acc[:],
+                    lhsT=fc[(g, hg)][:, j * P : (j + 1) * P].bitcast(E5M2),
+                    lhsT_scale=fs[(g, hg)][:, j * P : (j + 1) * P],
+                    rhs=wc[:, hg, half * 256 : half * 256 + 512].bitcast(E4M3),
+                    rhs_scale=ws[:, hg, half * 256 : half * 256 + 512],
+                    start=(k == ks[0]),
+                    stop=(k == ks[-1]),
+                )
+            cols = slice(0, 512) if half == 0 else slice(512, 768)
+            src = acc[:] if half == 0 else acc[:, 256:512]
+
+            def fin(copy):
+                if ks[0] == 0:
+                    if half == 0:
+                        dxo[(g, j)] = work.tile([P, D], F32, name="dxo", tag="dxo", bufs=3)
+                    copy(out=dxo[(g, j)][:, cols], in_=src)
+                else:
+                    o = dxo[(g, j)]
+                    nc.vector.tensor_tensor(out=o[:, cols], in0=src, in1=o[:, cols], op=ALU.add)
+                    if half == 1:
+                        nc.sync.dma_start(out=dx_v[g][:, j, :], in_=o[:])
+
+            return fin
+
+
+        un = {n: {} for n in range(10)}
+
+        def v_u(n):
+            g, hg = units[n]
+            c = tab[(g, "q" if hg < 4 else "k")][0]
+            u = work.tile([P, 2048], F32, name="u", tag="u", bufs=1)
+            nc.vector.tensor_tensor(
+                out=u[:].rearrange("p (j h f) -> p h j f", j=4, h=4),
+                in0=gt[n][:].rearrange("p h (j f) -> p h j f", f=HD),
+                in1=c[:].unsqueeze(1).to_broadcast([P, 4, 4, HD]),
+                op=ALU.mult,
+            )
+            un[n]["u"] = u
+            un[n]["v"] = work.tile([P, 2048], F32, name="v", tag="v", bufs=1)
+
+        def v_v(n, h):
+            g, hg = units[n]
+            s = tab[(g, "q" if hg < 4 else "k")][1]
+            nc.vector.tensor_tensor(
+                out=un[n]["v"][:].rearrange("p (j h f) -> p h j f", j=4, h=4)[:, h],
+                in0=gt[n][:, h, :].rearrange("p (j f) -> p j f", f=HD),
+                in1=s[:],
+                op=ALU.mult,
+            )
+
+        def v_dn(n):
+            dn = work.tile([P, 16, 16, 8], F32, name="dn", tag="dn", bufs=3)
+            uv = un[n]["u"][:].rearrange("p (b a c) -> p a b c", b=16, a=16)
+            vv = un[n]["v"][:].rearrange("p (b a c) -> p a b c", b=16, a=16)
+            nc.vector.tensor_tensor(out=dn[:, 0:8], in0=uv[:, 0:8], in1=vv[:, 8:16], op=ALU.add)
+            nc.vector.tensor_tensor(out=dn[:, 8:16], in0=uv[:, 8:16], in1=vv[:, 0:8], op=ALU.add)
+            un[n]["dn"] = dn
+
+        def v_p(n):
+            zv = zt[n][:].rearrange("p j c -> p (j c)").rearrange("p (b a c) -> p a b c", b=16, a=16)
+            pv = un[n]["v"][:].rearrange("p (a b c) -> p a b c", a=16, b=16)
+            nc.vector.tensor_tensor(out=pv, in0=un[n]["dn"][:], in1=zv, op=ALU.mult)
+
+        def s_square(n):
+            q = work.tile([P, 16], F32, name="q2", tag="q2", bufs=2)
+            junk = work.tile([P, 4, HD], BF16, name="junk", tag="junk", bufs=1)
+            for b in range(16):
+                j, h = b // 4, b % 4
+                cols = slice(h * HD, (h + 1) * HD)
+                nc.scalar.activation(
+                    out=junk[:, b % 4, :], in_=zt[n][:, j, cols], func=ACT.Square, accum_out=q[:, b : b + 1]
+                )
+            un[n]["q2"] = q
+
+        def pe_sum(n, slot, flat, step):
+            if slot == 0:
+                un[n]["stat"] = ps.tile([P, 3, P], F32, name="stat", tag="stat", bufs=1)
+            out = un[n]["stat"][:, slot, :]
+            for a in range(16):
+                src = flat[:, a::16] if step else flat[:, a * P : (a + 1) * P]
+                nc.tensor.matmul(out=out, lhsT=src, rhs=ident[:], start=(a == 0), stop=(a == 15), is_transpose=True)
+
+        def pe_z(n):
+            pe_sum(n, 0, zt[n][:].rearrange("p j c -> p (j c)"), True)
+
+        def pe_dn(n):
+            pe_sum(n, 1, un[n]["dn"][:].rearrange("p a b c -> p (a b c)"), False)
+
+        def pe_p(n):
+            pe_sum(n, 2, un[n]["v"][:], False)
+
+        def stats(n):
+            part = work.tile([P, 3, P], F32, name="part", tag="part", bufs=1)
+            nc.scalar.copy(out=part[:], in_=un[n]["stat"][:])
+            sm = ps.tile([P, 3, 16], F32, name="sm", tag="sm", bufs=1)
+            for k in range(3):
+                nc.tensor.matmul(out=sm[:, k, :], lhsT=part[:, k, :], rhs=sel[:], start=True, stop=True)
+            un[n]["sm"] = sm
+
+        def small_ops(n):
+            t = {}
+            for nm in ("mm", "var", "std", "r", "d", "f", "y", "r2", "A", "h", "i", "B"):
+                t[nm] = work.tile([P, 16], F32, name="s_" + nm, tag="s_" + nm, bufs=2)
+            st = work.tile([P, 3, 16], F32, name="st", tag="st", bufs=2)
+            un[n]["t"] = t
+            mu, m1, e2 = st[:, 0, :], st[:, 1, :], st[:, 2, :]
+
+            def tt(o, a, b, op):
+                return lambda: nc.vector.tensor_tensor(out=t[o][:], in0=a, in1=b, op=op)
+
+            def std():
+                nc.vector.scalar_tensor_tensor(
+                    out=t["var"][:], in0=un[n]["q2"][:], scalar=1.0 / HD, in1=t["mm"][:], op0=ALU.mult, op1=ALU.subtract
+                )
+                nc.scalar.activation(out=t["std"][:], in_=t["var"][:], func=ACT.Sqrt, bias=eps[:])
+
+            def b_op():
+                nc.vector.scalar_tensor_tensor(
+                    out=t["B"][:], in0=t["h"][:], scalar=-1.0, in1=t["i"][:], op0=ALU.mult, op1=ALU.subtract
+                )
+
+            return [
+                lambda: nc.vector.tensor_copy(out=st[:], in_=un[n]["sm"][:]),
+                tt("mm", mu, mu, ALU.mult),
+                tt("d", mu, m1, ALU.mult),
+                std,
+                tt("f", t["d"][:], e2, ALU.subtract),
+                lambda: nc.vector.reciprocal(out=t["r"][:], in_=t["std"][:]),
+                tt("y", t["r"][:], t["f"][:], ALU.mult),
+                tt("r2", t["r"][:], t["r"][:], ALU.mult),
+                tt("i", t["r"][:], m1, ALU.mult),
+                tt("A", t["r2"][:], t["y"][:], ALU.mult),
+                tt("h", t["A"][:], mu, ALU.mult),
+                b_op,
+            ]
+
+        def s_t(n):
+            t = un[n]["t"]
+            for h in range(4):
+                for j in range(4):
+                    b = j * 4 + h
+                    blk = zt[n][:, j, h * HD : (h + 1) * HD]
+                    nc.scalar.activation(
+                        out=blk, in_=blk, func=ACT.Identity, scale=t["A"][:, b : b + 1], bias=t["B"][:, b : b + 1]
+                    )
+
+        def v_fin(n, h):
+            t = un[n]["t"]
+            if h == 0:
+                un[n]["dz"] = work.tile([P, 4, 512], BF16, name="dz", tag="dz", bufs=2)
+            for j in range(4):
+                b = j * 4 + h
+                cols = slice(h * HD, (h + 1) * HD)
+                nc.vector.scalar_tensor_tensor(
+                    out=un[n]["dz"][:, j, cols].rearrange("p (a c) -> p a c", c=8),
+                    in0=un[n]["dn"][:, :, b, :],
+                    scalar=t["r"][:, b : b + 1],
+                    in1=zt[n][:, j, cols].rearrange("p (a c) -> p a c", c=8),
+                    op0=ALU.mult,
+                    op1=ALU.add,
+                )
+
+        w_jobs = [(dp, hg) for dp in range(3) for hg in range(NH)]
+        w_plan = {1: 3, 2: 3, 3: 3, 4: 3, 5: 3, 6: 3}
+        dw = lambda hg, lo, hi: [(dw_job, (hg, d)) for d in range(lo, hi)]
+        dx0 = [(dx_job, (0, j, half)) for j in range(4) for half in range(2)]
+        mx_plan = {
+            2: dw(5, 0, 2), 3: dw(5, 2, 4), 4: dw(5, 4, 6), 5: dw(0, 0, 2), 6: dw(0, 2, 4), 7: dw(0, 4, 6),
+            8: dx0[0:4], 9: dx0[4:8] + dw(1, 0, 2),
+        }
+
+        def run_mx(jobs, engines="S"):
+            for lo in range(0, len(jobs), 4):
+                done = [fn(*args) for fn, args in jobs[lo : lo + 4]]
+                for i, f in enumerate(done):
+                    f(nc.vector.tensor_copy if engines[(lo + i) % len(engines)] == "V" else nc.scalar.copy)
+
+        w_chunks = [(dp, c) for dp in range(3) for c in range(3)]
+        load_gamma("q", q_gamma)
+        load_cs(0)
+        load_unit(0)
+        dvt = {0: load_dv(0)}
+        load_x(0)
+        load_cs(1)
+        load_unit(1)
+        load_w(*w_chunks[0])
+        load_w(*w_chunks[1])
+        load_gamma("k", k_gamma)
+        dvt[1] = load_dv(1)
+        w_loaded = 2
+
+        with tc.manual_schedule(engines={mybir.EngineType.PE, mybir.EngineType.Activation, mybir.EngineType.DVE}):
+            swap_gamma("q")
+            make_tables(0, "q")
+            w_next = 0
+            deferred = []
+            for n in range(10):
+                a = n - 1 if n >= 1 else None
+                b = n - 2 if n >= 2 else None
+                small = []
+                if a is not None:
+                    pe_p(a)
+                    stats(a)
+                    small = small_ops(a)
+                if b is not None:
+                    for h in range(4):
+                        v_fin(b, h)
+                s_square(n)
+                for f in deferred:
+                    f()
+                deferred = []
+                v_u(n)
+                banks = None
+                if b is not None:
+                    il = work.tile([P, 512, 4], BF16, name="il", tag="q", bufs=3, align_bytes=64)
+                    banks = f_transposes(un[b]["dz"])
+                    for h in range(2):
+                        hc = slice(h * HD, (h + 1) * HD)
+                        interleave(nc.scalar.copy, il[:, hc, :], un[b]["dz"][:, :, hc])
+                pe_z(n)
+                for k in range(4):
+                    for f in small[k * 3 : k * 3 + 3]:
+                        f()
+                    v_v(n, k)
+                if b is not None:
+                    for h in range(2, 4):
+                        hc = slice(h * HD, (h + 1) * HD)
+                        interleave(nc.scalar.copy, il[:, hc, :], un[b]["dz"][:, :, hc])
+                    xt = f_copies(banks)
+                if n in (0, 1):
+                    deferred.append(dv_unit(n, dvt[n]))
+                    prep_x(n)
+                    if n == 0:
+                        load_x(1)
+                run_mx(mx_plan.get(n, []))
+                for i in range(w_plan.get(n, 0)):
+                    deferred.append(w_job(*w_jobs[w_next]))
+                    w_next += 1
+                while w_loaded < 9 and w_loaded < w_next // 2 + (2 if n == 0 else 4):
+                    load_w(*w_chunks[w_loaded])
+                    w_loaded += 1
+                deferred += xq
+                xq.clear()
+                if a is not None:
+                    s_t(a)
+                v_dn(n)
+                pe_dn(n)
+                if b is not None:
+                    g, hg = units[b]
+                    quant_t(g, hg, il)
+                    quant_f(g, hg, xt)
+                v_p(n)
+                if n + 2 < 10:
+                    load_unit(n + 2)
+                if n == 0:
+                    make_tables(1, "q")
+                if n == 4:
+                    swap_gamma("k")
+                    make_tables(0, "k")
+                if n == 8:
+                    make_tables(1, "k")
+
+            def il_half(n, il, hs, copy):
+                for h in hs:
+                    hc = slice(h * HD, (h + 1) * HD)
+                    interleave(copy, il[:, hc, :], un[n]["dz"][:, :, hc])
+
+            def finish(n, mid):
+                il = work.tile([P, 512, 4], BF16, name="il", tag="q", bufs=3, align_bytes=64)
+                for h in range(4):
+                    v_fin(n, h)
+                banks = f_transposes(un[n]["dz"])
+                il_half(n, il, (0,), nc.scalar.copy)
+                mid()
+                il_half(n, il, (1, 2, 3), nc.vector.tensor_copy)
+                xt = f_copies(banks, nc.vector.tensor_copy)
+                g, hg = units[n]
+                quant_f(g, hg, xt)
+                quant_t(g, hg, il)
+
+            pe_p(9)
+            stats(9)
+            first = [fn(*args) for fn, args in dw(1, 2, 6)]
+
+            def mid8():
+                for f in small_ops(9):
+                    f()
+                s_t(9)
+                for f in first:
+                    f(nc.scalar.copy)
+
+            finish(8, mid8)
+            pj = [(j, half) for j in range(2, 4) for half in range(2)]
+            done = [dx_part(1, j, half, (0, 1, 2, 3)) for j, half in pj]
+            for i, f in enumerate(done):
+                f(nc.vector.tensor_copy if i % 2 else nc.scalar.copy)
+            run_mx(dw(2, 0, 4), "SSVS")
+            finish(9, lambda: None)
+            run_mx(dw(2, 4, 6), "SV")
+            opened = [dx_open(1, j, half) for j in range(2) for half in range(2)]
+            for i, f in enumerate(opened):
+                f()(nc.vector.tensor_copy if i % 2 else nc.scalar.copy)
+            run_mx(dw(3, 0, 2), "SV")
+            done = [dx_part(1, j, half, (4, 5)) for j, half in pj]
+            for f in done:
+                f(None)
+            run_mx(dw(3, 2, 6) + dw(4, 0, 6), "SV")

@@ -360,13 +360,13 @@ def tile_gqa_flashattn_pa_v_kernel(
             un[n]["u"] = u
             un[n]["v"] = work.tile([P, 2048], F32, name="v", tag="v", bufs=1)
 
-        def v_v(n, h):
+        def v_v(n):
             g, hg = units[n]
             s = tab[(g, "q" if hg < 4 else "k")][1]
             nc.vector.tensor_tensor(
-                out=un[n]["v"][:].rearrange("p (j h f) -> p h j f", j=4, h=4)[:, h],
-                in0=gt[n][:, h, :].rearrange("p (j f) -> p j f", f=HD),
-                in1=s[:],
+                out=un[n]["v"][:].rearrange("p (j h f) -> p h j f", j=4, h=4),
+                in0=gt[n][:].rearrange("p h (j f) -> p h j f", f=HD),
+                in1=s[:].unsqueeze(1).to_broadcast([P, 4, 4, HD]),
                 op=ALU.mult,
             )
 
@@ -421,40 +421,30 @@ def tile_gqa_flashattn_pa_v_kernel(
 
         def small_ops(n):
             t = {}
-            for nm in ("mm", "var", "std", "r", "d", "f", "y", "r2", "A", "h", "i", "B"):
+            for nm in ("qe", "mm", "ve", "rho", "r", "d", "f", "y", "A", "h", "i", "B"):
                 t[nm] = work.tile([P, 16], F32, name="s_" + nm, tag="s_" + nm, bufs=2)
             st = work.tile([P, 3, 16], F32, name="st", tag="st", bufs=2)
             un[n]["t"] = t
             mu, m1, e2 = st[:, 0, :], st[:, 1, :], st[:, 2, :]
 
             def tt(o, a, b, op):
-                return lambda: nc.vector.tensor_tensor(out=t[o][:], in0=a, in1=b, op=op)
+                nc.vector.tensor_tensor(out=t[o][:], in0=a, in1=b, op=op)
 
-            def std():
-                nc.vector.scalar_tensor_tensor(
-                    out=t["var"][:], in0=un[n]["q2"][:], scalar=1.0 / HD, in1=t["mm"][:], op0=ALU.mult, op1=ALU.subtract
-                )
-                nc.scalar.activation(out=t["std"][:], in_=t["var"][:], func=ACT.Sqrt, bias=eps[:])
-
-            def b_op():
-                nc.vector.scalar_tensor_tensor(
-                    out=t["B"][:], in0=t["h"][:], scalar=-1.0, in1=t["i"][:], op0=ALU.mult, op1=ALU.subtract
-                )
-
-            return [
-                lambda: nc.vector.tensor_copy(out=st[:], in_=un[n]["sm"][:]),
-                tt("mm", mu, mu, ALU.mult),
-                tt("d", mu, m1, ALU.mult),
-                std,
-                tt("f", t["d"][:], e2, ALU.subtract),
-                lambda: nc.vector.reciprocal(out=t["r"][:], in_=t["std"][:]),
-                tt("y", t["r"][:], t["f"][:], ALU.mult),
-                tt("r2", t["r"][:], t["r"][:], ALU.mult),
-                tt("i", t["r"][:], m1, ALU.mult),
-                tt("A", t["r2"][:], t["y"][:], ALU.mult),
-                tt("h", t["A"][:], mu, ALU.mult),
-                b_op,
-            ]
+            nc.scalar.activation(out=t["qe"][:], in_=un[n]["q2"][:], func=ACT.Identity, scale=1.0 / HD, bias=eps[:])
+            nc.scalar.copy(out=st[:], in_=un[n]["sm"][:])
+            nc.scalar.activation(out=t["mm"][:], in_=mu, func=ACT.Square)
+            tt("d", mu, m1, ALU.mult)
+            tt("ve", t["qe"][:], t["mm"][:], ALU.subtract)
+            tt("f", t["d"][:], e2, ALU.subtract)
+            nc.vector.reciprocal(out=t["rho"][:], in_=t["ve"][:])
+            nc.scalar.activation(out=t["r"][:], in_=t["rho"][:], func=ACT.Sqrt)
+            tt("y", t["rho"][:], t["f"][:], ALU.mult)
+            tt("A", t["r"][:], t["y"][:], ALU.mult)
+            tt("i", t["r"][:], m1, ALU.mult)
+            tt("h", t["A"][:], mu, ALU.mult)
+            nc.vector.scalar_tensor_tensor(
+                out=t["B"][:], in0=t["h"][:], scalar=-1.0, in1=t["i"][:], op0=ALU.mult, op1=ALU.subtract
+            )
 
         def s_t(n):
             t = un[n]["t"]
@@ -511,7 +501,7 @@ def tile_gqa_flashattn_pa_v_kernel(
         dvt[1] = load_dv(1)
         w_loaded = 2
 
-        with tc.manual_schedule(engines={mybir.EngineType.PE, mybir.EngineType.Activation, mybir.EngineType.DVE}):
+        if True:
             swap_gamma("q")
             make_tables(0, "q")
             w_next = 0
@@ -519,11 +509,9 @@ def tile_gqa_flashattn_pa_v_kernel(
             for n in range(10):
                 a = n - 1 if n >= 1 else None
                 b = n - 2 if n >= 2 else None
-                small = []
                 if a is not None:
                     pe_p(a)
                     stats(a)
-                    small = small_ops(a)
                 if b is not None:
                     for h in range(4):
                         v_fin(b, h)
@@ -540,10 +528,9 @@ def tile_gqa_flashattn_pa_v_kernel(
                         hc = slice(h * HD, (h + 1) * HD)
                         interleave(nc.scalar.copy, il[:, hc, :], un[b]["dz"][:, :, hc])
                 pe_z(n)
-                for k in range(4):
-                    for f in small[k * 3 : k * 3 + 3]:
-                        f()
-                    v_v(n, k)
+                if a is not None:
+                    small_ops(a)
+                v_v(n)
                 if b is not None:
                     for h in range(2, 4):
                         hc = slice(h * HD, (h + 1) * HD)
@@ -605,8 +592,7 @@ def tile_gqa_flashattn_pa_v_kernel(
             first = [fn(*args) for fn, args in dw(1, 2, 6)]
 
             def mid8():
-                for f in small_ops(9):
-                    f()
+                small_ops(9)
                 s_t(9)
                 for f in first:
                     f(nc.scalar.copy)

from contextlib import ExitStack

import concourse.mybir as mybir
from concourse.masks import make_identity

F32 = mybir.dt.float32
BF16 = mybir.dt.bfloat16
U32 = mybir.dt.uint32
U8 = mybir.dt.uint8
E4M3 = mybir.dt.float8_e4m3fn_x4
E5M2 = mybir.dt.float8_e5m2_x4
ALU = mybir.AluOpType
ACT = mybir.ActivationFunctionType
AX = mybir.AxisListType

P = 128
T = 1024
D = 768
HD = 128
EPS = 1e-6
NG = 2
NH = 6
FLOPS = 2 * 2 * T * D * 3072


def tile_gqa_flashattn_pa_v_kernel(
    tc, x, cos, sin, wq, wk, wv, q_gamma, q_beta, k_gamma, k_beta, zq, zk, grad_0, grad_1, grad_2,
    out_0, out_1, out_2, out_3,
):
    nc = tc.nc
    x_v = x[0].rearrange("(g p j) d -> g p j d", p=P, j=4)
    cos_v = cos.rearrange("(g p j) f -> g p j f", p=P, j=4)
    sin_v = sin.rearrange("(g p j) f -> g p j f", p=P, j=4)
    zq_v = zq[0].rearrange("(g p j) c -> g p j c", p=P, j=4)
    zk_v = zk[0].rearrange("(g p j) c -> g p j c", p=P, j=4)
    g0_v = grad_0[0].rearrange("h (g p j) f -> g p h (j f)", p=P, j=4)
    g1_v = grad_1[0].rearrange("h (g p j) f -> g p h (j f)", p=P, j=4)
    g2_v = grad_2[0].rearrange("h (g p j) f -> g h p j f", p=P, j=4)
    dx_v = out_0[0].rearrange("(g p j) d -> g p j d", p=P, j=4)

    def z_src(g, hg):
        return zq_v[g][:, :, hg * 512 : (hg + 1) * 512] if hg < 4 else zk_v[g]

    def g_src(g, hg):
        return g0_v[g][:, hg * 4 : hg * 4 + 4, :] if hg < 4 else g1_v[g]

    def dw_dst(hg, d):
        rows = slice(d * P, (d + 1) * P)
        if hg < 4:
            return out_1[rows, hg * 512 : (hg + 1) * 512]
        return out_2[rows, :] if hg == 4 else out_3[rows, :]

    with ExitStack() as ctx:
        const = ctx.enter_context(tc.tile_pool(name="const", bufs=1))
        work = ctx.enter_context(tc.tile_pool(name="work", bufs=3))
        codes = ctx.enter_context(tc.tile_pool(name="codes", bufs=1))
        ps = ctx.enter_context(tc.psum_pool(name="ps", bufs=1))

        ident = const.tile([P, P], F32, name="ident")
        make_identity(nc, ident[:])
        sel = const.tile([P, 16], F32, name="sel")
        sel1 = const.tile([P, 16], F32, name="sel1")
        nc.vector.tensor_reduce(out=sel1[:], in_=ident[:].rearrange("p (n e) -> p n e", e=8), axis=AX.X, op=ALU.add)
        nc.vector.tensor_scalar(out=sel[:], in0=sel1[:], scalar1=1.0 / HD, scalar2=None, op0=ALU.mult)
        zero = const.tile([P, 1], F32, name="zero")
        nc.vector.memset(zero[:], 0.0)
        eps = const.tile([P, 1], F32, name="eps")
        nc.vector.tensor_scalar(out=eps[:], in0=zero[:], scalar1=EPS, scalar2=None, op0=ALU.add)

        units = [(0, 0), (1, 0), (0, 1), (0, 2), (0, 3), (0, 4), (1, 1), (1, 2), (1, 3), (1, 4)]
        cosr = [None, None]
        sinr = [None, None]
        gam = {}
        gsw = {}
        tab = {}
        zt = {}
        gt = {}

        def load_cs(g):
            a = const.tile([P, 4, HD], BF16, name="cosr%d" % g)
            nc.sync.dma_start(out=a[:], in_=cos_v[g])
            b = const.tile([P, 4, HD], BF16, name="sinr%d" % g)
            nc.sync.dma_start(out=b[:], in_=sin_v[g])
            cosr[g] = a
            sinr[g] = b

        def load_gamma(kind, src):
            a = const.tile([P, HD], BF16, name="gam_" + kind, tag="gam_" + kind)
            nc.sync.dma_start(out=a[:], in_=src.partition_broadcast(P))
            gam[kind] = a

        def swap_gamma(kind):
            a = gam[kind]
            b = const.tile([P, HD], BF16, name="gsw_" + kind, tag="gsw_" + kind)
            nc.vector.tensor_scalar(out=b[:, 0:64], in0=a[:, 64:128], scalar1=-1.0, scalar2=None, op0=ALU.mult)
            nc.vector.tensor_copy(out=b[:, 64:128], in_=a[:, 0:64])
            gsw[kind] = b

        def make_tables(g, kind):
            a, b = gam[kind], gsw[kind]
            c = const.tile([P, 4, HD], F32, name="tab_c%d" % g)
            s = const.tile([P, 4, HD], F32, name="tab_s%d" % g)
            nc.vector.tensor_tensor(out=c[:], in0=cosr[g][:], in1=a[:].unsqueeze(1).to_broadcast([P, 4, HD]), op=ALU.mult)
            nc.vector.tensor_tensor(out=s[:], in0=sinr[g][:], in1=b[:].unsqueeze(1).to_broadcast([P, 4, HD]), op=ALU.mult)
            tab[(g, kind)] = (c, s)

        def load_unit(n):
            g, hg = units[n]
            b = work.tile([P, 4, 512], BF16, name="gt", tag="gt", bufs=2)
            nc.sync.dma_start(out=b[:], in_=g_src(g, hg))
            a = work.tile([P, 4, 512], F32, name="zt", tag="zt", bufs=4)
            nc.sync.dma_start(out=a[:], in_=z_src(g, hg))
            gt[n] = b
            zt[n] = a

        xc = codes.tile([P, NG, D], U32, name="xc", align_bytes=64)
        xs = codes.tile([P, NG, D], U8, name="xs", align_bytes=64)
        wc = codes.tile([P, NH, D], U32, name="wc", align_bytes=64)
        ws = codes.tile([P, NH, D], U8, name="ws", align_bytes=64)
        fc = {}
        fs = {}
        tcd = {}
        tsc = {}
        for hg in range(NH):
            for g in range(NG):
                fc[(g, hg)] = codes.tile([P, 512], U32, name="fc%d_%d" % (g, hg), align_bytes=64)
                fs[(g, hg)] = codes.tile([P, 512], U8, name="fs%d_%d" % (g, hg), align_bytes=64)

        def token_codes(g, hg):
            tcd[(g, hg)] = work.tile([P, 512], U32, name="tcod", tag="tcod", bufs=6, align_bytes=64)
            tsc[(g, hg)] = work.tile([P, 512], U8, name="tsca", tag="tsca", bufs=6, align_bytes=64)
            return tcd[(g, hg)], tsc[(g, hg)]

        def interleave(engine_copy, dst, src):
            engine_copy(
                out=dst.rearrange("p (c i) t -> p c t i", i=4),
                in_=src.rearrange("p t (c i) -> p c t i", i=4),
            )

        xraw = {}

        def load_x(g):
            for lo, w in ((0, 512), (512, 256)):
                raw = work.tile([P, 4, w], BF16, name="raw", tag="raw", bufs=4)
                nc.sync.dma_start(out=raw[:], in_=x_v[g][:, :, lo : lo + w])
                xraw[(g, lo)] = raw

        def prep_x(g):
            for lo, w, tag, bufs in ((0, 512, "q", 3), (512, 256, "wil", 4)):
                il = work.tile([P, w, 4], BF16, name="xil", tag=tag, bufs=bufs, align_bytes=64)
                interleave(nc.scalar.copy, il[:], xraw[(g, lo)][:])
                yield_q(g, lo, w, il)

        xq = []

        def yield_q(g, lo, w, il):
            def f():
                nc.vector.quantize_mx(
                    out=xc[:, g, lo : lo + w].bitcast(E4M3),
                    scales=xs[:, g, lo : lo + w],
                    in_=il[:].rearrange("p c j -> p (c j)"),
                )

            xq.append(f)

        wraw = {}

        def load_w(dp, c):
            raw = work.tile([P, 2, 1024], BF16, name="raw", tag="raw", bufs=4)
            rows = slice(dp * 256, dp * 256 + 256)
            if c < 2:
                nc.sync.dma_start(
                    out=raw[:], in_=wq[rows, c * 1024 : (c + 1) * 1024].rearrange("(k p) e -> p k e", p=P)
                )
            else:
                nc.sync.dma_start(out=raw[:, :, 0:512], in_=wk[rows, :].rearrange("(k p) e -> p k e", p=P))
                nc.sync.dma_start(out=raw[:, :, 512:1024], in_=wv[rows, :].rearrange("(k p) e -> p k e", p=P))
            wraw[(dp, c)] = raw

        def w_job(dp, hg):
            bank = ps.tile([P, 2, 2, P], F32, name="tr", tag="tr", bufs=2)
            for k in range(2):
                words = wraw[(dp, hg // 2)][:, k, :].bitcast(F32)
                lo = (hg % 2) * 256
                for u in range(2):
                    nc.tensor.transpose(bank[:, k, u, :], words[:, lo + u : lo + 256 : 2], ident[:])
            il = work.tile([P, 2, P, 4], BF16, name="wil", tag="wil", bufs=4, align_bytes=64)
            nc.scalar.copy(
                out=il[:].rearrange("p k r e -> p (k r e)").bitcast(F32).rearrange("p (k r u) -> p k r u", k=2, u=2),
                in_=bank[:].rearrange("p k u r -> p k r u"),
            )

            def fin():
                cols = slice(dp * 256, dp * 256 + 256)
                nc.vector.quantize_mx(
                    out=wc[:, hg, cols].bitcast(E4M3),
                    scales=ws[:, hg, cols],
                    in_=il[:].rearrange("p k r e -> p (k r e)"),
                )

            return fin

        def f_transposes(dz):
            banks = []
            for jp in range(2):
                bank = ps.tile([P, 2, 2, P], F32, name="tr", tag="tr", bufs=2)
                for k in range(2):
                    words = dz[:, jp * 2 + k, :].bitcast(F32)
                    for u in range(2):
                        nc.tensor.transpose(bank[:, k, u, :], words[:, u:256:2], ident[:])
                banks.append(bank)
            return banks

        def f_copies(banks, second=nc.scalar.copy):
            xt = work.tile([P, 4, P, 4], BF16, name="xt", tag="q", bufs=3, align_bytes=64)
            for jp in range(2):
                dst = xt[:, jp * 2 : jp * 2 + 2].rearrange("p k r e -> p (k r e)").bitcast(F32)
                (second if jp else nc.scalar.copy)(
                    out=dst.rearrange("p (k r u) -> p k r u", k=2, u=2),
                    in_=banks[jp][:].rearrange("p k u r -> p k r u"),
                )
            return xt

        def quant_f(g, hg, xt):
            nc.vector.quantize_mx(
                out=fc[(g, hg)][:].bitcast(E5M2), scales=fs[(g, hg)][:], in_=xt[:].rearrange("p k r e -> p (k r e)")
            )

        def quant_t(g, hg, il):
            c, s = token_codes(g, hg)
            nc.vector.quantize_mx(out=c[:].bitcast(E5M2), scales=s[:], in_=il[:].rearrange("p c j -> p (c j)"))

        def load_dv(g):
            dz = work.tile([P, 4, 512], BF16, name="dz", tag="dz", bufs=2)
            for h in range(4):
                nc.sync.dma_start(out=dz[:, :, h * HD : (h + 1) * HD], in_=g2_v[g][h])
            return dz

        def dv_unit(g, dz):
            il = work.tile([P, 512, 4], BF16, name="il", tag="q", bufs=3, align_bytes=64)
            interleave(nc.scalar.copy, il[:], dz[:])
            xt = f_copies(f_transposes(dz))

            def fin():
                quant_t(g, 5, il)
                quant_f(g, 5, xt)

            return fin

        dwn = [0]
        dwt = {}

        def dw_job(hg, d):
            acc = ps.tile([P, 512], F32, name="mm", tag="mm", bufs=4)
            for g in range(NG):
                nc.tensor.matmul_mx(
                    out=acc[:],
                    lhsT=xc[:, g, d * P : (d + 1) * P].bitcast(E4M3),
                    lhsT_scale=xs[:, g, d * P : (d + 1) * P],
                    rhs=tcd[(g, hg)][:].bitcast(E5M2),
                    rhs_scale=tsc[(g, hg)][:],
                    start=(g == 0),
                    stop=(g == NG - 1),
                )

            def fin(copy):
                if hg in (5, 0):
                    o = work.tile([P, 512], F32, name="dwo", tag="dwo", bufs=4)[:]
                else:
                    if dwn[0] % 2 == 0:
                        dwt[0] = work.tile([P, 2, 512], F32, name="dwo2", tag="raw", bufs=4)
                    o = dwt[0][:, dwn[0] % 2, :]
                    dwn[0] += 1
                copy(out=o, in_=acc[:])
                nc.sync.dma_start(out=dw_dst(hg, d), in_=o)

            return fin

        dxo = {}
        order = (5, 0, 1, 2, 3, 4)

        def dx_open(g, j, half, tag="mm", bufs=4):
            acc = ps.tile([P, 512], F32, name="mm", tag=tag, bufs=bufs)

            def mm(k, start, stop):
                hg = order[k]
                nc.tensor.matmul_mx(
                    out=acc[:],
                    lhsT=fc[(g, hg)][:, j * P : (j + 1) * P].bitcast(E5M2),
                    lhsT_scale=fs[(g, hg)][:, j * P : (j + 1) * P],
                    rhs=wc[:, hg, half * 256 : half * 256 + 512].bitcast(E4M3),
                    rhs_scale=ws[:, hg, half * 256 : half * 256 + 512],
                    start=start,
                    stop=stop,
                )

            for k in range(5):
                mm(k, k == 0, False)

            def close():
                mm(5, False, True)

                def fin(copy):
                    if half == 0:
                        dxo[(g, j)] = work.tile([P, D], F32, name="dxo", tag="dxo", bufs=3)
                        copy(out=dxo[(g, j)][:, 0:512], in_=acc[:])
                    else:
                        copy(out=dxo[(g, j)][:, 512:768], in_=acc[:, 256:512])
                        nc.sync.dma_start(out=dx_v[g][:, j, :], in_=dxo[(g, j)][:])

                return fin

            return close

        def dx_job(g, j, half):
            return dx_open(g, j, half)()

        def dx_part(g, j, half, ks):
            acc = ps.tile([P, 512], F32, name="mm", tag="mm", bufs=4)
            for k in ks:
                hg = order[k]
                nc.tensor.matmul_mx(
                    out=acc[:],
                    lhsT=fc[(g, hg)][:, j * P : (j + 1) * P].bitcast(E5M2),
                    lhsT_scale=fs[(g, hg)][:, j * P : (j + 1) * P],
                    rhs=wc[:, hg, half * 256 : half * 256 + 512].bitcast(E4M3),
                    rhs_scale=ws[:, hg, half * 256 : half * 256 + 512],
                    start=(k == ks[0]),
                    stop=(k == ks[-1]),
                )
            cols = slice(0, 512) if half == 0 else slice(512, 768)
            src = acc[:] if half == 0 else acc[:, 256:512]

            def fin(copy):
                if ks[0] == 0:
                    if half == 0:
                        dxo[(g, j)] = work.tile([P, D], F32, name="dxo", tag="dxo", bufs=3)
                    copy(out=dxo[(g, j)][:, cols], in_=src)
                else:
                    o = dxo[(g, j)]
                    nc.vector.tensor_tensor(out=o[:, cols], in0=src, in1=o[:, cols], op=ALU.add)
                    if half == 1:
                        nc.sync.dma_start(out=dx_v[g][:, j, :], in_=o[:])

            return fin


        un = {n: {} for n in range(10)}

        def v_u(n):
            g, hg = units[n]
            c = tab[(g, "q" if hg < 4 else "k")][0]
            u = work.tile([P, 2048], F32, name="u", tag="u", bufs=1)
            nc.vector.tensor_tensor(
                out=u[:].rearrange("p (j h f) -> p h j f", j=4, h=4),
                in0=gt[n][:].rearrange("p h (j f) -> p h j f", f=HD),
                in1=c[:].unsqueeze(1).to_broadcast([P, 4, 4, HD]),
                op=ALU.mult,
            )
            un[n]["u"] = u
            un[n]["v"] = work.tile([P, 2048], F32, name="v", tag="v", bufs=1)

        def v_v(n):
            g, hg = units[n]
            s = tab[(g, "q" if hg < 4 else "k")][1]
            nc.vector.tensor_tensor(
                out=un[n]["v"][:].rearrange("p (j h f) -> p h j f", j=4, h=4),
                in0=gt[n][:].rearrange("p h (j f) -> p h j f", f=HD),
                in1=s[:].unsqueeze(1).to_broadcast([P, 4, 4, HD]),
                op=ALU.mult,
            )

        def v_dn(n):
            dn = work.tile([P, 16, 16, 8], F32, name="dn", tag="dn", bufs=3)
            uv = un[n]["u"][:].rearrange("p (b a c) -> p a b c", b=16, a=16)
            vv = un[n]["v"][:].rearrange("p (b a c) -> p a b c", b=16, a=16)
            nc.vector.tensor_tensor(out=dn[:, 0:8], in0=uv[:, 0:8], in1=vv[:, 8:16], op=ALU.add)
            nc.vector.tensor_tensor(out=dn[:, 8:16], in0=uv[:, 8:16], in1=vv[:, 0:8], op=ALU.add)
            un[n]["dn"] = dn

        def v_p(n):
            zv = zt[n][:].rearrange("p j c -> p (j c)").rearrange("p (b a c) -> p a b c", b=16, a=16)
            pv = un[n]["v"][:].rearrange("p (a b c) -> p a b c", a=16, b=16)
            nc.vector.tensor_tensor(out=pv, in0=un[n]["dn"][:], in1=zv, op=ALU.mult)

        def s_square(n):
            q = work.tile([P, 16], F32, name="q2", tag="q2", bufs=2)
            junk = work.tile([P, 4, HD], BF16, name="junk", tag="junk", bufs=1)
            for b in range(16):
                j, h = b // 4, b % 4
                cols = slice(h * HD, (h + 1) * HD)
                nc.scalar.activation(
                    out=junk[:, b % 4, :], in_=zt[n][:, j, cols], func=ACT.Square, accum_out=q[:, b : b + 1]
                )
            un[n]["q2"] = q

        def pe_sum(n, slot, flat, step):
            if slot == 0:
                un[n]["stat"] = ps.tile([P, 3, P], F32, name="stat", tag="stat", bufs=1)
            out = un[n]["stat"][:, slot, :]
            for a in range(16):
                src = flat[:, a::16] if step else flat[:, a * P : (a + 1) * P]
                nc.tensor.matmul(out=out, lhsT=src, rhs=ident[:], start=(a == 0), stop=(a == 15), is_transpose=True)

        def pe_z(n):
            pe_sum(n, 0, zt[n][:].rearrange("p j c -> p (j c)"), True)

        def pe_dn(n):
            pe_sum(n, 1, un[n]["dn"][:].rearrange("p a b c -> p (a b c)"), False)

        def pe_p(n):
            pe_sum(n, 2, un[n]["v"][:], False)

        def stats(n):
            part = work.tile([P, 3, P], F32, name="part", tag="part", bufs=1)
            nc.scalar.copy(out=part[:], in_=un[n]["stat"][:])
            sm = ps.tile([P, 3, 16], F32, name="sm", tag="sm", bufs=1)
            for k in range(3):
                nc.tensor.matmul(out=sm[:, k, :], lhsT=part[:, k, :], rhs=sel[:], start=True, stop=True)
            un[n]["sm"] = sm

        def small_ops(n):
            t = {}
            for nm in ("qe", "mm", "ve", "rho", "r", "d", "f", "y", "A", "h", "i", "B"):
                t[nm] = work.tile([P, 16], F32, name="s_" + nm, tag="s_" + nm, bufs=2)
            st = work.tile([P, 3, 16], F32, name="st", tag="st", bufs=2)
            un[n]["t"] = t
            mu, m1, e2 = st[:, 0, :], st[:, 1, :], st[:, 2, :]

            def tt(o, a, b, op):
                nc.vector.tensor_tensor(out=t[o][:], in0=a, in1=b, op=op)

            nc.scalar.activation(out=t["qe"][:], in_=un[n]["q2"][:], func=ACT.Identity, scale=1.0 / HD, bias=eps[:])
            nc.scalar.copy(out=st[:], in_=un[n]["sm"][:])
            nc.scalar.activation(out=t["mm"][:], in_=mu, func=ACT.Square)
            tt("d", mu, m1, ALU.mult)
            tt("ve", t["qe"][:], t["mm"][:], ALU.subtract)
            tt("f", t["d"][:], e2, ALU.subtract)
            nc.vector.reciprocal(out=t["rho"][:], in_=t["ve"][:])
            nc.scalar.activation(out=t["r"][:], in_=t["rho"][:], func=ACT.Sqrt)
            tt("y", t["rho"][:], t["f"][:], ALU.mult)
            tt("A", t["r"][:], t["y"][:], ALU.mult)
            tt("i", t["r"][:], m1, ALU.mult)
            tt("h", t["A"][:], mu, ALU.mult)
            nc.vector.scalar_tensor_tensor(
                out=t["B"][:], in0=t["h"][:], scalar=-1.0, in1=t["i"][:], op0=ALU.mult, op1=ALU.subtract
            )

        def s_t(n):
            t = un[n]["t"]
            for h in range(4):
                for j in range(4):
                    b = j * 4 + h
                    blk = zt[n][:, j, h * HD : (h + 1) * HD]
                    nc.scalar.activation(
                        out=blk, in_=blk, func=ACT.Identity, scale=t["A"][:, b : b + 1], bias=t["B"][:, b : b + 1]
                    )

        def v_fin(n, h):
            t = un[n]["t"]
            if h == 0:
                un[n]["dz"] = work.tile([P, 4, 512], BF16, name="dz", tag="dz", bufs=2)
            for j in range(4):
                b = j * 4 + h
                cols = slice(h * HD, (h + 1) * HD)
                nc.vector.scalar_tensor_tensor(
                    out=un[n]["dz"][:, j, cols].rearrange("p (a c) -> p a c", c=8),
                    in0=un[n]["dn"][:, :, b, :],
                    scalar=t["r"][:, b : b + 1],
                    in1=zt[n][:, j, cols].rearrange("p (a c) -> p a c", c=8),
                    op0=ALU.mult,
                    op1=ALU.add,
                )

        w_jobs = [(dp, hg) for dp in range(3) for hg in range(NH)]
        w_plan = {1: 3, 2: 3, 3: 3, 4: 3, 5: 3, 6: 3}
        dw = lambda hg, lo, hi: [(dw_job, (hg, d)) for d in range(lo, hi)]
        dx0 = [(dx_job, (0, j, half)) for j in range(4) for half in range(2)]
        mx_plan = {
            2: dw(5, 0, 2), 3: dw(5, 2, 4), 4: dw(5, 4, 6), 5: dw(0, 0, 2), 6: dw(0, 2, 4), 7: dw(0, 4, 6),
            8: dx0[0:4], 9: dx0[4:8] + dw(1, 0, 2),
        }

        def run_mx(jobs, engines="S"):
            for lo in range(0, len(jobs), 4):
                done = [fn(*args) for fn, args in jobs[lo : lo + 4]]
                for i, f in enumerate(done):
                    f(nc.vector.tensor_copy if engines[(lo + i) % len(engines)] == "V" else nc.scalar.copy)

        w_chunks = [(dp, c) for dp in range(3) for c in range(3)]
        load_gamma("q", q_gamma)
        load_cs(0)
        load_unit(0)
        dvt = {0: load_dv(0)}
        load_x(0)
        load_cs(1)
        load_unit(1)
        load_w(*w_chunks[0])
        load_w(*w_chunks[1])
        load_gamma("k", k_gamma)
        dvt[1] = load_dv(1)
        w_loaded = 2

        if True:
            swap_gamma("q")
            make_tables(0, "q")
            w_next = 0
            deferred = []
            for n in range(10):
                a = n - 1 if n >= 1 else None
                b = n - 2 if n >= 2 else None
                if a is not None:
                    pe_p(a)
                    stats(a)
                if b is not None:
                    for h in range(4):
                        v_fin(b, h)
                s_square(n)
                for f in deferred:
                    f()
                deferred = []
                v_u(n)
                banks = None
                if b is not None:
                    il = work.tile([P, 512, 4], BF16, name="il", tag="q", bufs=3, align_bytes=64)
                    banks = f_transposes(un[b]["dz"])
                    for h in range(2):
                        hc = slice(h * HD, (h + 1) * HD)
                        interleave(nc.scalar.copy, il[:, hc, :], un[b]["dz"][:, :, hc])
                pe_z(n)
                if a is not None:
                    small_ops(a)
                v_v(n)
                if b is not None:
                    for h in range(2, 4):
                        hc = slice(h * HD, (h + 1) * HD)
                        interleave(nc.scalar.copy, il[:, hc, :], un[b]["dz"][:, :, hc])
                    xt = f_copies(banks)
                if n in (0, 1):
                    deferred.append(dv_unit(n, dvt[n]))
                    prep_x(n)
                    if n == 0:
                        load_x(1)
                run_mx(mx_plan.get(n, []))
                for i in range(w_plan.get(n, 0)):
                    deferred.append(w_job(*w_jobs[w_next]))
                    w_next += 1
                while w_loaded < 9 and w_loaded < w_next // 2 + (2 if n == 0 else 4):
                    load_w(*w_chunks[w_loaded])
                    w_loaded += 1
                deferred += xq
                xq.clear()
                if a is not None:
                    s_t(a)
                v_dn(n)
                pe_dn(n)
                if b is not None:
                    g, hg = units[b]
                    quant_t(g, hg, il)
                    quant_f(g, hg, xt)
                v_p(n)
                if n + 2 < 10:
                    load_unit(n + 2)
                if n == 0:
                    make_tables(1, "q")
                if n == 4:
                    swap_gamma("k")
                    make_tables(0, "k")
                if n == 8:
                    make_tables(1, "k")

            def il_half(n, il, hs, copy):
                for h in hs:
                    hc = slice(h * HD, (h + 1) * HD)
                    interleave(copy, il[:, hc, :], un[n]["dz"][:, :, hc])

            def finish(n, mid):
                il = work.tile([P, 512, 4], BF16, name="il", tag="q", bufs=3, align_bytes=64)
                for h in range(4):
                    v_fin(n, h)
                banks = f_transposes(un[n]["dz"])
                il_half(n, il, (0,), nc.scalar.copy)
                mid()
                il_half(n, il, (1, 2, 3), nc.vector.tensor_copy)
                xt = f_copies(banks, nc.vector.tensor_copy)
                g, hg = units[n]
                quant_f(g, hg, xt)
                quant_t(g, hg, il)

            pe_p(9)
            stats(9)
            first = [fn(*args) for fn, args in dw(1, 2, 6)]

            def mid8():
                small_ops(9)
                s_t(9)
                for f in first:
                    f(nc.scalar.copy)

            finish(8, mid8)
            pj = [(j, half) for j in range(2, 4) for half in range(2)]
            done = [dx_part(1, j, half, (0, 1, 2, 3)) for j, half in pj]
            for i, f in enumerate(done):
                f(nc.vector.tensor_copy if i % 2 else nc.scalar.copy)
            run_mx(dw(2, 0, 4), "SSVS")
            finish(9, lambda: None)
            run_mx(dw(2, 4, 6), "SV")
            opened = [dx_open(1, j, half) for j in range(2) for half in range(2)]
            for i, f in enumerate(opened):
                f()(nc.vector.tensor_copy if i % 2 else nc.scalar.copy)
            run_mx(dw(3, 0, 2), "SV")
            done = [dx_part(1, j, half, (4, 5)) for j, half in pj]
            for f in done:
                f(None)
            run_mx(dw(3, 2, 6) + dw(4, 0, 6), "SV")
